import numpy as np
import ml_dtypes


def mxq(x, axis, fmt="e4m3"):
    dtype, down = {"e4m3": (ml_dtypes.float8_e4m3fn, 7), "e5m2": (ml_dtypes.float8_e5m2, 14)}[fmt]
    v = np.moveaxis(np.asarray(x, np.float32).astype(ml_dtypes.bfloat16).astype(np.float64), axis, -1)
    blocks = v.reshape(v.shape[:-1] + (-1, 32))
    amax = np.abs(blocks).max(-1, keepdims=True)
    byte = np.maximum(np.where(amax > 0, np.frexp(amax)[1] - 1 + 127, 0) - down, 1)
    scale = np.exp2(byte - 127.0)
    codes = (blocks / scale).astype(np.float32).astype(dtype).astype(np.float64)
    return np.moveaxis((codes * scale).reshape(v.shape), -1, axis)


WIDE = False


def mx_kscale(k):
    if not WIDE:
        return np.ones(k)
    levels = np.array([10, -10, 5, -5, 0])
    a = np.random.permutation(np.resize(levels, k // 512 * 4)).reshape(k // 512, 4)
    idx = np.arange(k)
    return np.exp2(a[idx // 512, idx % 128 // 32])


BF16 = ml_dtypes.bfloat16


def bf(x):
    return np.asarray(x, np.float32).astype(BF16)


def f64(x):
    return np.asarray(x).astype(np.float64)


B, N, C, DIN, H, KS, KC = 8, 512, 4, 64, 64, 3, 3


def setup_inputs():
    s = mx_kscale(N)
    sn = s[None, :, None, None]
    return {"Gs": bf(np.random.standard_normal((N, N)) * 0.5 / np.sqrt(N) * s[None, :] / s[:, None]),
            "Xt": bf(np.random.standard_normal((B, N, C, DIN)) * sn),
            "Ht_1": bf(np.random.standard_normal((B, N, C, H)) * sn)}


def reference(Gs, Xt, Ht_1):
    g = f64(Gs)
    g0 = mxq(g, 0, "e4m3")
    t2 = 2.0 * (mxq(g, 1, "e4m3") @ g0) - np.eye(N)
    xh = np.concatenate([f64(Xt), f64(Ht_1)], axis=-1)
    xq = mxq(xh.transpose(0, 2, 3, 1), 3, "e4m3")
    x1 = (xq @ g0).transpose(0, 3, 1, 2)
    x2 = (xq @ mxq(t2, 0, "e4m3")).transpose(0, 3, 1, 2)
    return x1, x2

@@ -1,0 +1,168 @@
+from contextlib import ExitStack
+
+import concourse.mybir as mybir
+from concourse.masks import make_identity
+
+BF16 = mybir.dt.bfloat16
+F32 = mybir.dt.float32
+U32 = mybir.dt.uint32
+U8 = mybir.dt.uint8
+FP8X4 = mybir.dt.float8_e4m3fn_x4
+MULT = mybir.AluOpType.mult
+SUBTRACT = mybir.AluOpType.subtract
+
+P = 128
+PACK = 4
+BATCH = 8
+NODES = P * PACK
+CHANNELS = 4
+DIN = 64
+SOURCES = 2
+HALF = CHANNELS * DIN
+WIDTH = SOURCES * HALF
+RUN = 4
+
+FLOPS = 2 * NODES * NODES * NODES + 2 * (2 * BATCH * WIDTH * NODES * NODES)
+
+
+def tile_stc_cell_pa_t_kernel(tc, Gs, Xt, Ht_1, out_0, out_1):
+    nc = tc.nc
+    with ExitStack() as stack:
+        keep = stack.enter_context(tc.tile_pool(name="keep", bufs=1))
+        stage = stack.enter_context(tc.tile_pool(name="stage", bufs=3))
+        results = stack.enter_context(tc.tile_pool(name="results", bufs=6))
+        psum = stack.enter_context(tc.psum_pool(name="psum", bufs=8))
+        stack.enter_context(tc.manual_schedule())
+
+        def quarter(i):
+            return slice(i * P, (i + 1) * P)
+
+        g_rows = keep.tile([P, PACK, NODES], BF16)
+        nc.sync.dma_start(out=g_rows[:], in_=Gs.rearrange("(p j) m -> p j m", j=PACK))
+        xh_rows = keep.tile([P, BATCH, SOURCES, PACK, HALF], BF16)
+        for b in range(BATCH):
+            for s, source in enumerate((Xt, Ht_1)):
+                nc.sync.dma_start(
+                    out=xh_rows[:, b, s, :, :],
+                    in_=source[b].rearrange("(p j) c d -> p j (c d)", j=PACK),
+                )
+
+        ident = keep.tile([P, P], F32)
+        make_identity(nc, ident[:])
+        eye_grouped = keep.tile([P, PACK, P, PACK], F32)
+        nc.vector.memset(eye_grouped[:], 0.0)
+        for i in range(PACK):
+            nc.vector.tensor_copy(out=eye_grouped[:, i, :, i], in_=ident[:])
+
+        g_grouped = keep.tile([P, PACK, P, PACK], BF16, align_bytes=64)
+        nc.vector.tensor_copy(
+            out=g_grouped[:], in_=g_rows[:].rearrange("p j (r i) -> p i r j", i=PACK)
+        )
+        g_codes = keep.tile([P, NODES], U32, align_bytes=64)
+        g_scales = keep.tile([P, NODES], U8, align_bytes=64)
+
+        gt_grouped = keep.tile([P, PACK * P * PACK], BF16, align_bytes=64)
+        gt_words = gt_grouped[:].bitcast(F32).rearrange("q (j r u) -> q j r u", j=PACK, u=2)
+        for half in range(2):
+            flipped = psum.tile([P, 2, 2, P], F32, tag="bank")
+            for jj in range(2):
+                words = g_rows[:, 2 * half + jj, :].bitcast(F32).rearrange("r (q u) -> r u q", u=2)
+                for u in range(2):
+                    nc.tensor.transpose(flipped[:, jj, u, :], words[:, u, :], ident[:])
+            nc.scalar.copy(
+                out=gt_words[:, 2 * half : 2 * half + 2, :, :],
+                in_=flipped[:].rearrange("q j u r -> q j r u"),
+            )
+        gt_codes = keep.tile([P, NODES], U32, align_bytes=64)
+        gt_scales = keep.tile([P, NODES], U8, align_bytes=64)
+
+        t2_grouped = keep.tile([P, PACK, P, PACK], BF16, align_bytes=64)
+        t2_codes = keep.tile([P, NODES], U32, align_bytes=64)
+        t2_scales = keep.tile([P, NODES], U8, align_bytes=64)
+
+        def chebyshev(i):
+            square = psum.tile([P, PACK, P], F32, tag="bank")
+            for j in range(PACK):
+                nc.tensor.matmul_mx(
+                    out=square[:, j, :],
+                    lhsT=gt_codes[:, quarter(j)].bitcast(FP8X4),
+                    lhsT_scale=gt_scales[:, quarter(j)],
+                    rhs=g_codes[:, quarter(i)].bitcast(FP8X4),
+                    rhs_scale=g_scales[:, quarter(i)],
+                    start=True,
+                    stop=True,
+                )
+            nc.vector.scalar_tensor_tensor(
+                out=t2_grouped[:, i, :, :],
+                in0=square[:].rearrange("r j c -> r c j"),
+                scalar=2.0,
+                in1=eye_grouped[:, i, :, :],
+                op0=MULT,
+                op1=SUBTRACT,
+            )
+            nc.vector.quantize_mx(
+                out=t2_codes[:, quarter(i)].bitcast(FP8X4),
+                scales=t2_scales[:, quarter(i)],
+                in_=t2_grouped[:, i, :, :].rearrange("r c j -> r (c j)"),
+            )
+
+        xh_codes = keep.tile([P, BATCH, WIDTH], U32, align_bytes=64)
+        xh_scales = keep.tile([P, BATCH, WIDTH], U8, align_bytes=64)
+
+        def regroup_features(b):
+            xh_grouped = stage.tile([P, SOURCES, HALF, PACK], BF16, align_bytes=64)
+            for s in range(SOURCES):
+                nc.vector.tensor_copy(
+                    out=xh_grouped[:, s, :, :].rearrange("p (w i) j -> p w j i", i=RUN),
+                    in_=xh_rows[:, b, s, :, :].rearrange("p j (w i) -> p w j i", i=RUN),
+                )
+            return xh_grouped
+
+        def quantise_features(b, xh_grouped):
+            nc.vector.quantize_mx(
+                out=xh_codes[:, b, :].bitcast(FP8X4),
+                scales=xh_scales[:, b, :],
+                in_=xh_grouped[:].rearrange("p s w j -> p (s w j)"),
+            )
+
+        def diffuse(b, codes, scales, out, vector_banks):
+            result = results.tile([P, PACK, CHANNELS, SOURCES, DIN], F32)
+            for i in range(PACK):
+                acc = psum.tile([P, WIDTH], F32, tag="bank")
+                nc.tensor.matmul_mx(
+                    out=acc[:],
+                    lhsT=codes[:, quarter(i)].bitcast(FP8X4),
+                    lhsT_scale=scales[:, quarter(i)],
+                    rhs=xh_codes[:, b, :].bitcast(FP8X4),
+                    rhs_scale=xh_scales[:, b, :],
+                    start=True,
+                    stop=True,
+                )
+                columns = acc[:].rearrange("r (s c d) -> r c s d", s=SOURCES, c=CHANNELS)
+                if i < vector_banks:
+                    nc.vector.tensor_copy(out=result[:, i], in_=columns)
+                else:
+                    nc.scalar.copy(out=result[:, i], in_=columns)
+            nc.sync.dma_start(
+                out=out[b].rearrange("(r i) c l -> r (i c l)", i=PACK),
+                in_=result[:].rearrange("r i c s d -> r (i c s d)"),
+            )
+
+        first_grouped = regroup_features(0)
+        nc.vector.quantize_mx(
+            out=g_codes[:].bitcast(FP8X4),
+            scales=g_scales[:],
+            in_=g_grouped[:].rearrange("p i r j -> p (i r j)"),
+        )
+        quantise_features(0, first_grouped)
+        nc.vector.quantize_mx(out=gt_codes[:].bitcast(FP8X4), scales=gt_scales[:], in_=gt_grouped[:])
+        for b in range(BATCH + 1):
+            if b + 1 < BATCH:
+                quantise_features(b + 1, regroup_features(b + 1))
+            if b < BATCH:
+                diffuse(b, g_codes, g_scales, out_0, vector_banks=0)
+            if b == 0:
+                for i in range(PACK):
+                    chebyshev(i)
+            else:
+                diffuse(b - 1, t2_codes, t2_scales, out_1, vector_banks=2)

@@ -100,6 +100,8 @@ def tile_stc_cell_pa_t_kernel(tc, Gs, Xt, Ht_1, out_0, out_1):
                 op0=MULT,
                 op1=SUBTRACT,
             )
+
+        def quantise_chebyshev(i):
             nc.vector.quantize_mx(
                 out=t2_codes[:, quarter(i)].bitcast(FP8X4),
                 scales=t2_scales[:, quarter(i)],
@@ -148,6 +150,12 @@ def tile_stc_cell_pa_t_kernel(tc, Gs, Xt, Ht_1, out_0, out_1):
                 in_=result[:].rearrange("r i c s d -> r (i c s d)"),
             )
 
+        def x1(b):
+            diffuse(b, g_codes, g_scales, out_0, vector_banks=0)
+
+        def x2(b):
+            diffuse(b, t2_codes, t2_scales, out_1, vector_banks=2)
+
         first_grouped = regroup_features(0)
         nc.vector.quantize_mx(
             out=g_codes[:].bitcast(FP8X4),
@@ -156,13 +164,19 @@ def tile_stc_cell_pa_t_kernel(tc, Gs, Xt, Ht_1, out_0, out_1):
         )
         quantise_features(0, first_grouped)
         nc.vector.quantize_mx(out=gt_codes[:].bitcast(FP8X4), scales=gt_scales[:], in_=gt_grouped[:])
-        for b in range(BATCH + 1):
+        quantise_features(1, regroup_features(1))
+        x1(0)
+        for i in range(PACK + 1):
+            if i < PACK:
+                chebyshev(i)
+            if i > 0:
+                quantise_chebyshev(i - 1)
+        x1(1)
+        quantise_features(2, regroup_features(2))
+        x2(0)
+        x2(1)
+        for b in range(2, BATCH):
             if b + 1 < BATCH:
                 quantise_features(b + 1, regroup_features(b + 1))
-            if b < BATCH:
-                diffuse(b, g_codes, g_scales, out_0, vector_banks=0)
-            if b == 0:
-                for i in range(PACK):
-                    chebyshev(i)
-            else:
-                diffuse(b - 1, t2_codes, t2_scales, out_1, vector_banks=2)
+            x1(b)
+            x2(b)

@@ -164,19 +164,19 @@ def tile_stc_cell_pa_t_kernel(tc, Gs, Xt, Ht_1, out_0, out_1):
         )
         quantise_features(0, first_grouped)
         nc.vector.quantize_mx(out=gt_codes[:].bitcast(FP8X4), scales=gt_scales[:], in_=gt_grouped[:])
-        quantise_features(1, regroup_features(1))
         x1(0)
+        quantise_features(1, regroup_features(1))
         for i in range(PACK + 1):
             if i < PACK:
                 chebyshev(i)
             if i > 0:
                 quantise_chebyshev(i - 1)
         x1(1)
-        quantise_features(2, regroup_features(2))
         x2(0)
+        quantise_features(2, regroup_features(2))
         x2(1)
         for b in range(2, BATCH):
+            x1(b)
             if b + 1 < BATCH:
                 quantise_features(b + 1, regroup_features(b + 1))
-            x1(b)
             x2(b)

@@ -55,32 +55,31 @@ def tile_stc_cell_pa_t_kernel(tc, Gs, Xt, Ht_1, out_0, out_1):
             nc.vector.tensor_copy(out=eye_grouped[:, i, :, i], in_=ident[:])
 
         g_grouped = keep.tile([P, PACK, P, PACK], BF16, align_bytes=64)
-        nc.vector.tensor_copy(
-            out=g_grouped[:], in_=g_rows[:].rearrange("p j (r i) -> p i r j", i=PACK)
-        )
         g_codes = keep.tile([P, NODES], U32, align_bytes=64)
         g_scales = keep.tile([P, NODES], U8, align_bytes=64)
 
         gt_grouped = keep.tile([P, PACK * P * PACK], BF16, align_bytes=64)
         gt_words = gt_grouped[:].bitcast(F32).rearrange("q (j r u) -> q j r u", j=PACK, u=2)
-        for half in range(2):
-            flipped = psum.tile([P, 2, 2, P], F32, tag="bank")
-            for jj in range(2):
-                words = g_rows[:, 2 * half + jj, :].bitcast(F32).rearrange("r (q u) -> r u q", u=2)
-                for u in range(2):
-                    nc.tensor.transpose(flipped[:, jj, u, :], words[:, u, :], ident[:])
-            nc.scalar.copy(
-                out=gt_words[:, 2 * half : 2 * half + 2, :, :],
-                in_=flipped[:].rearrange("q j u r -> q j r u"),
-            )
         gt_codes = keep.tile([P, NODES], U32, align_bytes=64)
         gt_scales = keep.tile([P, NODES], U8, align_bytes=64)
+
+        def flip_graph():
+            for half in range(2):
+                flipped = psum.tile([P, 2, 2, P], F32, tag="bank")
+                for jj in range(2):
+                    words = g_rows[:, 2 * half + jj, :].bitcast(F32).rearrange("r (q u) -> r u q", u=2)
+                    for u in range(2):
+                        nc.tensor.transpose(flipped[:, jj, u, :], words[:, u, :], ident[:])
+                nc.scalar.copy(
+                    out=gt_words[:, 2 * half : 2 * half + 2, :, :],
+                    in_=flipped[:].rearrange("q j u r -> q j r u"),
+                )
 
         t2_grouped = keep.tile([P, PACK, P, PACK], BF16, align_bytes=64)
         t2_codes = keep.tile([P, NODES], U32, align_bytes=64)
         t2_scales = keep.tile([P, NODES], U8, align_bytes=64)
 
-        def chebyshev(i):
+        def square_graph(i):
             square = psum.tile([P, PACK, P], F32, tag="bank")
             for j in range(PACK):
                 nc.tensor.matmul_mx(
@@ -92,6 +91,9 @@ def tile_stc_cell_pa_t_kernel(tc, Gs, Xt, Ht_1, out_0, out_1):
                     start=True,
                     stop=True,
                 )
+            return square
+
+        def chebyshev(i, square):
             nc.vector.scalar_tensor_tensor(
                 out=t2_grouped[:, i, :, :],
                 in0=square[:].rearrange("r j c -> r c j"),
@@ -111,14 +113,11 @@ def tile_stc_cell_pa_t_kernel(tc, Gs, Xt, Ht_1, out_0, out_1):
         xh_codes = keep.tile([P, BATCH, WIDTH], U32, align_bytes=64)
         xh_scales = keep.tile([P, BATCH, WIDTH], U8, align_bytes=64)
 
-        def regroup_features(b):
-            xh_grouped = stage.tile([P, SOURCES, HALF, PACK], BF16, align_bytes=64)
-            for s in range(SOURCES):
-                nc.vector.tensor_copy(
-                    out=xh_grouped[:, s, :, :].rearrange("p (w i) j -> p w j i", i=RUN),
-                    in_=xh_rows[:, b, s, :, :].rearrange("p j (w i) -> p w j i", i=RUN),
-                )
-            return xh_grouped
+        def regroup_source(b, s, xh_grouped, copy):
+            copy(
+                out=xh_grouped[:, s, :, :].rearrange("p (w i) j -> p w j i", i=RUN),
+                in_=xh_rows[:, b, s, :, :].rearrange("p j (w i) -> p w j i", i=RUN),
+            )
 
         def quantise_features(b, xh_grouped):
             nc.vector.quantize_mx(
@@ -127,8 +126,14 @@ def tile_stc_cell_pa_t_kernel(tc, Gs, Xt, Ht_1, out_0, out_1):
                 in_=xh_grouped[:].rearrange("p s w j -> p (s w j)"),
             )
 
-        def diffuse(b, codes, scales, out, vector_banks):
-            result = results.tile([P, PACK, CHANNELS, SOURCES, DIN], F32)
+        def prepare(b):
+            xh_grouped = stage.tile([P, SOURCES, HALF, PACK], BF16, align_bytes=64)
+            for s in range(SOURCES):
+                regroup_source(b, s, xh_grouped, nc.vector.tensor_copy)
+            quantise_features(b, xh_grouped)
+
+        def passes(b, codes, scales):
+            banks = []
             for i in range(PACK):
                 acc = psum.tile([P, WIDTH], F32, tag="bank")
                 nc.tensor.matmul_mx(
@@ -140,43 +145,70 @@ def tile_stc_cell_pa_t_kernel(tc, Gs, Xt, Ht_1, out_0, out_1):
                     start=True,
                     stop=True,
                 )
-                columns = acc[:].rearrange("r (s c d) -> r c s d", s=SOURCES, c=CHANNELS)
-                if i < vector_banks:
-                    nc.vector.tensor_copy(out=result[:, i], in_=columns)
-                else:
-                    nc.scalar.copy(out=result[:, i], in_=columns)
-            nc.sync.dma_start(
-                out=out[b].rearrange("(r i) c l -> r (i c l)", i=PACK),
-                in_=result[:].rearrange("r i c s d -> r (i c s d)"),
+                banks.append(acc)
+            return banks
+
+        def empty(banks, result, i, copy):
+            copy(
+                out=result[:, i],
+                in_=banks[i][:].rearrange("r (s c d) -> r c s d", s=SOURCES, c=CHANNELS),
             )
 
+        def store(out, b, result, first, count):
+            span = slice(first * WIDTH, (first + count) * WIDTH)
+            nc.sync.dma_start(
+                out=out[b].rearrange("(r i) c l -> r (i c l)", i=PACK)[:, span],
+                in_=result[:].rearrange("r i c s d -> r (i c s d)")[:, span],
+            )
+
+        def leave(out, b, banks, vector_banks, pieces=1):
+            result = results.tile([P, PACK, CHANNELS, SOURCES, DIN], F32)
+            step = PACK // pieces
+            for i in range(PACK):
+                empty(banks, result, i, nc.vector.tensor_copy if i < vector_banks else nc.scalar.copy)
+                if (i + 1) % step == 0:
+                    store(out, b, result, i + 1 - step, step)
+
         def x1(b):
-            diffuse(b, g_codes, g_scales, out_0, vector_banks=0)
+            return passes(b, g_codes, g_scales)
 
         def x2(b):
-            diffuse(b, t2_codes, t2_scales, out_1, vector_banks=2)
+            return passes(b, t2_codes, t2_scales)
 
-        first_grouped = regroup_features(0)
+        nc.vector.tensor_copy(
+            out=g_grouped[:], in_=g_rows[:].rearrange("p j (r i) -> p i r j", i=PACK)
+        )
+        first_grouped = stage.tile([P, SOURCES, HALF, PACK], BF16, align_bytes=64, tag="xh_grouped")
+        regroup_source(0, 0, first_grouped, nc.scalar.copy)
+        flip_graph()
+        regroup_source(0, 1, first_grouped, nc.vector.tensor_copy)
         nc.vector.quantize_mx(
             out=g_codes[:].bitcast(FP8X4),
             scales=g_scales[:],
             in_=g_grouped[:].rearrange("p i r j -> p (i r j)"),
         )
         quantise_features(0, first_grouped)
+        leave(out_0, 0, x1(0), 0, pieces=2)
+        second_grouped = stage.tile([P, SOURCES, HALF, PACK], BF16, align_bytes=64, tag="xh_grouped")
+        for s in range(SOURCES):
+            regroup_source(1, s, second_grouped, nc.vector.tensor_copy)
         nc.vector.quantize_mx(out=gt_codes[:].bitcast(FP8X4), scales=gt_scales[:], in_=gt_grouped[:])
-        x1(0)
-        quantise_features(1, regroup_features(1))
+        quantise_features(1, second_grouped)
+        squares = [square_graph(0), square_graph(1)]
+        x1_banks = x1(1)
+        squares.extend([square_graph(2), square_graph(3)])
         for i in range(PACK + 1):
             if i < PACK:
-                chebyshev(i)
+                chebyshev(i, squares[i])
             if i > 0:
                 quantise_chebyshev(i - 1)
-        x1(1)
-        x2(0)
-        quantise_features(2, regroup_features(2))
-        x2(1)
+        leave(out_0, 1, x1_banks, 0)
+        x2_banks = [x2(0), x2(1)]
+        leave(out_1, 0, x2_banks[0], 2)
+        prepare(2)
+        leave(out_1, 1, x2_banks[1], 0)
         for b in range(2, BATCH):
-            x1(b)
+            leave(out_0, b, x1(b), 0)
             if b + 1 < BATCH:
-                quantise_features(b + 1, regroup_features(b + 1))
-            x2(b)
+                prepare(b + 1)
+            leave(out_1, b, x2(b), 2)

@@ -49,7 +49,7 @@ def tile_stc_cell_pa_t_kernel(tc, Gs, Xt, Ht_1, out_0, out_1):
 
         ident = keep.tile([P, P], F32)
         make_identity(nc, ident[:])
-        eye_grouped = keep.tile([P, PACK, P, PACK], F32)
+        eye_grouped = keep.tile([P, PACK, P, PACK], BF16)
         nc.vector.memset(eye_grouped[:], 0.0)
         for i in range(PACK):
             nc.vector.tensor_copy(out=eye_grouped[:, i, :, i], in_=ident[:])
@@ -165,7 +165,7 @@ def tile_stc_cell_pa_t_kernel(tc, Gs, Xt, Ht_1, out_0, out_1):
             result = results.tile([P, PACK, CHANNELS, SOURCES, DIN], F32)
             step = PACK // pieces
             for i in range(PACK):
-                empty(banks, result, i, nc.vector.tensor_copy if i < vector_banks else nc.scalar.copy)
+                empty(banks, result, i, nc.vector.tensor_copy if i in vector_banks else nc.scalar.copy)
                 if (i + 1) % step == 0:
                     store(out, b, result, i + 1 - step, step)
 
@@ -176,11 +176,14 @@ def tile_stc_cell_pa_t_kernel(tc, Gs, Xt, Ht_1, out_0, out_1):
             return passes(b, t2_codes, t2_scales)
 
         nc.vector.tensor_copy(
-            out=g_grouped[:], in_=g_rows[:].rearrange("p j (r i) -> p i r j", i=PACK)
+            out=g_grouped[:].rearrange("p i r j -> p r j i"),
+            in_=g_rows[:].rearrange("p j (r i) -> p r j i", i=PACK),
         )
         first_grouped = stage.tile([P, SOURCES, HALF, PACK], BF16, align_bytes=64, tag="xh_grouped")
+        second_grouped = stage.tile([P, SOURCES, HALF, PACK], BF16, align_bytes=64, tag="xh_grouped")
         regroup_source(0, 0, first_grouped, nc.scalar.copy)
         flip_graph()
+        regroup_source(1, 0, second_grouped, nc.scalar.copy)
         regroup_source(0, 1, first_grouped, nc.vector.tensor_copy)
         nc.vector.quantize_mx(
             out=g_codes[:].bitcast(FP8X4),
@@ -188,27 +191,24 @@ def tile_stc_cell_pa_t_kernel(tc, Gs, Xt, Ht_1, out_0, out_1):
             in_=g_grouped[:].rearrange("p i r j -> p (i r j)"),
         )
         quantise_features(0, first_grouped)
-        leave(out_0, 0, x1(0), 0, pieces=2)
-        second_grouped = stage.tile([P, SOURCES, HALF, PACK], BF16, align_bytes=64, tag="xh_grouped")
-        for s in range(SOURCES):
-            regroup_source(1, s, second_grouped, nc.vector.tensor_copy)
+        leave(out_0, 0, x1(0), (), pieces=2)
+        regroup_source(1, 1, second_grouped, nc.vector.tensor_copy)
         nc.vector.quantize_mx(out=gt_codes[:].bitcast(FP8X4), scales=gt_scales[:], in_=gt_grouped[:])
         quantise_features(1, second_grouped)
-        squares = [square_graph(0), square_graph(1)]
+        squares = [square_graph(i) for i in range(PACK)]
         x1_banks = x1(1)
-        squares.extend([square_graph(2), square_graph(3)])
         for i in range(PACK + 1):
             if i < PACK:
                 chebyshev(i, squares[i])
             if i > 0:
                 quantise_chebyshev(i - 1)
-        leave(out_0, 1, x1_banks, 0)
+        leave(out_0, 1, x1_banks, (), pieces=2)
         x2_banks = [x2(0), x2(1)]
-        leave(out_1, 0, x2_banks[0], 2)
+        leave(out_1, 0, x2_banks[0], (0, 2), pieces=2)
         prepare(2)
-        leave(out_1, 1, x2_banks[1], 0)
+        leave(out_1, 1, x2_banks[1], (), pieces=2)
         for b in range(2, BATCH):
-            leave(out_0, b, x1(b), 0)
+            leave(out_0, b, x1(b), (), pieces=2 if b == 2 else 1)
             if b + 1 < BATCH:
                 prepare(b + 1)
-            leave(out_1, b, x2(b), 2)
+            leave(out_1, b, x2(b), (0, 1))

@@ -37,9 +37,9 @@ def tile_stc_cell_pa_t_kernel(tc, Gs, Xt, Ht_1, out_0, out_1):
         def quarter(i):
             return slice(i * P, (i + 1) * P)
 
-        g_rows = keep.tile([P, PACK, NODES], BF16)
+        g_rows = keep.tile([P, PACK, NODES], BF16, align_bytes=256)
         nc.sync.dma_start(out=g_rows[:], in_=Gs.rearrange("(p j) m -> p j m", j=PACK))
-        xh_rows = keep.tile([P, BATCH, SOURCES, PACK, HALF], BF16)
+        xh_rows = keep.tile([P, BATCH, SOURCES, PACK, HALF], BF16, align_bytes=256)
         for b in range(BATCH):
             for s, source in enumerate((Xt, Ht_1)):
                 nc.sync.dma_start(
@@ -162,7 +162,7 @@ def tile_stc_cell_pa_t_kernel(tc, Gs, Xt, Ht_1, out_0, out_1):
             )
 
         def leave(out, b, banks, vector_banks, pieces=1):
-            result = results.tile([P, PACK, CHANNELS, SOURCES, DIN], F32)
+            result = results.tile([P, PACK, CHANNELS, SOURCES, DIN], F32, align_bytes=256)
             step = PACK // pieces
             for i in range(PACK):
                 empty(banks, result, i, nc.vector.tensor_copy if i in vector_banks else nc.scalar.copy)

@@ -204,11 +204,11 @@ def tile_stc_cell_pa_t_kernel(tc, Gs, Xt, Ht_1, out_0, out_1):
                 quantise_chebyshev(i - 1)
         leave(out_0, 1, x1_banks, (), pieces=2)
         x2_banks = [x2(0), x2(1)]
-        leave(out_1, 0, x2_banks[0], (0, 2), pieces=2)
+        leave(out_1, 0, x2_banks[0], (0, 2))
         prepare(2)
-        leave(out_1, 1, x2_banks[1], (), pieces=2)
+        leave(out_1, 1, x2_banks[1], ())
         for b in range(2, BATCH):
-            leave(out_0, b, x1(b), (), pieces=2 if b == 2 else 1)
+            leave(out_0, b, x1(b), ())
             if b + 1 < BATCH:
                 prepare(b + 1)
             leave(out_1, b, x2(b), (0, 1))

@@ -20,6 +20,7 @@ DIN = 64
 SOURCES = 2
 HALF = CHANNELS * DIN
 WIDTH = SOURCES * HALF
+PAIRS_FROM = 4
 RUN = 4
 
 FLOPS = 2 * NODES * NODES * NODES + 2 * (2 * BATCH * WIDTH * NODES * NODES)
@@ -31,6 +32,7 @@ def tile_stc_cell_pa_t_kernel(tc, Gs, Xt, Ht_1, out_0, out_1):
         keep = stack.enter_context(tc.tile_pool(name="keep", bufs=1))
         stage = stack.enter_context(tc.tile_pool(name="stage", bufs=3))
         results = stack.enter_context(tc.tile_pool(name="results", bufs=6))
+        doubles = stack.enter_context(tc.tile_pool(name="doubles", bufs=3))
         psum = stack.enter_context(tc.psum_pool(name="psum", bufs=8))
         stack.enter_context(tc.manual_schedule())
 
@@ -207,8 +209,34 @@ def tile_stc_cell_pa_t_kernel(tc, Gs, Xt, Ht_1, out_0, out_1):
         leave(out_1, 0, x2_banks[0], (0, 2))
         prepare(2)
         leave(out_1, 1, x2_banks[1], ())
-        for b in range(2, BATCH):
+        for b in range(2, PAIRS_FROM):
             leave(out_0, b, x1(b), ())
-            if b + 1 < BATCH:
-                prepare(b + 1)
+            prepare(b + 1)
             leave(out_1, b, x2(b), (0, 1))
+
+        def store_pair(out, b, double):
+            nc.sync.dma_start(
+                out=out[b : b + 2].rearrange("b (r i) c l -> r b (i c l)", i=PACK),
+                in_=double[:].rearrange("r b i c s d -> r b (i c s d)"),
+            )
+
+        for b in range(PAIRS_FROM, BATCH, 2):
+            double = doubles.tile([P, 2, PACK, CHANNELS, SOURCES, DIN], F32, align_bytes=256)
+            banks = x1(b)
+            prepare(b + 1)
+            for i in range(PACK):
+                empty(banks, double[:, 0], i, nc.scalar.copy)
+            banks = x1(b + 1)
+            for i in range(PACK):
+                empty(banks, double[:, 1], i, nc.scalar.copy)
+            store_pair(out_0, b, double)
+            double = doubles.tile([P, 2, PACK, CHANNELS, SOURCES, DIN], F32, align_bytes=256)
+            banks = x2(b)
+            for i in range(PACK):
+                empty(banks, double[:, 0], i, nc.vector.tensor_copy if i < 2 else nc.scalar.copy)
+            if b + 2 < BATCH:
+                prepare(b + 2)
+            banks = x2(b + 1)
+            for i in range(PACK):
+                empty(banks, double[:, 1], i, nc.vector.tensor_copy if i < 2 else nc.scalar.copy)
+            store_pair(out_1, b, double)

from contextlib import ExitStack

import concourse.mybir as mybir
from concourse.masks import make_identity

BF16 = mybir.dt.bfloat16
F32 = mybir.dt.float32
U32 = mybir.dt.uint32
U8 = mybir.dt.uint8
FP8X4 = mybir.dt.float8_e4m3fn_x4
MULT = mybir.AluOpType.mult
SUBTRACT = mybir.AluOpType.subtract

P = 128
PACK = 4
BATCH = 8
NODES = P * PACK
CHANNELS = 4
DIN = 64
SOURCES = 2
HALF = CHANNELS * DIN
WIDTH = SOURCES * HALF
PAIRS_FROM = 4
RUN = 4

FLOPS = 2 * NODES * NODES * NODES + 2 * (2 * BATCH * WIDTH * NODES * NODES)


def tile_stc_cell_pa_t_kernel(tc, Gs, Xt, Ht_1, out_0, out_1):
    nc = tc.nc
    with ExitStack() as stack:
        keep = stack.enter_context(tc.tile_pool(name="keep", bufs=1))
        stage = stack.enter_context(tc.tile_pool(name="stage", bufs=3))
        results = stack.enter_context(tc.tile_pool(name="results", bufs=6))
        doubles = stack.enter_context(tc.tile_pool(name="doubles", bufs=3))
        psum = stack.enter_context(tc.psum_pool(name="psum", bufs=8))
        stack.enter_context(tc.manual_schedule())

        def quarter(i):
            return slice(i * P, (i + 1) * P)

        g_rows = keep.tile([P, PACK, NODES], BF16, align_bytes=256)
        nc.sync.dma_start(out=g_rows[:], in_=Gs.rearrange("(p j) m -> p j m", j=PACK))
        xh_rows = keep.tile([P, BATCH, SOURCES, PACK, HALF], BF16, align_bytes=256)
        for b in range(BATCH):
            for s, source in enumerate((Xt, Ht_1)):
                nc.sync.dma_start(
                    out=xh_rows[:, b, s, :, :],
                    in_=source[b].rearrange("(p j) c d -> p j (c d)", j=PACK),
                )

        ident = keep.tile([P, P], F32)
        make_identity(nc, ident[:])
        eye_grouped = keep.tile([P, PACK, P, PACK], BF16)
        nc.vector.memset(eye_grouped[:], 0.0)
        for i in range(PACK):
            nc.vector.tensor_copy(out=eye_grouped[:, i, :, i], in_=ident[:])

        g_grouped = keep.tile([P, PACK, P, PACK], BF16, align_bytes=64)
        g_codes = keep.tile([P, NODES], U32, align_bytes=64)
        g_scales = keep.tile([P, NODES], U8, align_bytes=64)

        gt_grouped = keep.tile([P, PACK * P * PACK], BF16, align_bytes=64)
        gt_words = gt_grouped[:].bitcast(F32).rearrange("q (j r u) -> q j r u", j=PACK, u=2)
        gt_codes = keep.tile([P, NODES], U32, align_bytes=64)
        gt_scales = keep.tile([P, NODES], U8, align_bytes=64)

        def flip_graph():
            for half in range(2):
                flipped = psum.tile([P, 2, 2, P], F32, tag="bank")
                for jj in range(2):
                    words = g_rows[:, 2 * half + jj, :].bitcast(F32).rearrange("r (q u) -> r u q", u=2)
                    for u in range(2):
                        nc.tensor.transpose(flipped[:, jj, u, :], words[:, u, :], ident[:])
                nc.scalar.copy(
                    out=gt_words[:, 2 * half : 2 * half + 2, :, :],
                    in_=flipped[:].rearrange("q j u r -> q j r u"),
                )

        t2_grouped = keep.tile([P, PACK, P, PACK], BF16, align_bytes=64)
        t2_codes = keep.tile([P, NODES], U32, align_bytes=64)
        t2_scales = keep.tile([P, NODES], U8, align_bytes=64)

        def square_graph(i):
            square = psum.tile([P, PACK, P], F32, tag="bank")
            for j in range(PACK):
                nc.tensor.matmul_mx(
                    out=square[:, j, :],
                    lhsT=gt_codes[:, quarter(j)].bitcast(FP8X4),
                    lhsT_scale=gt_scales[:, quarter(j)],
                    rhs=g_codes[:, quarter(i)].bitcast(FP8X4),
                    rhs_scale=g_scales[:, quarter(i)],
                    start=True,
                    stop=True,
                )
            return square

        def chebyshev(i, square):
            nc.vector.scalar_tensor_tensor(
                out=t2_grouped[:, i, :, :],
                in0=square[:].rearrange("r j c -> r c j"),
                scalar=2.0,
                in1=eye_grouped[:, i, :, :],
                op0=MULT,
                op1=SUBTRACT,
            )

        def quantise_chebyshev(i):
            nc.vector.quantize_mx(
                out=t2_codes[:, quarter(i)].bitcast(FP8X4),
                scales=t2_scales[:, quarter(i)],
                in_=t2_grouped[:, i, :, :].rearrange("r c j -> r (c j)"),
            )

        xh_codes = keep.tile([P, BATCH, WIDTH], U32, align_bytes=64)
        xh_scales = keep.tile([P, BATCH, WIDTH], U8, align_bytes=64)

        def regroup_source(b, s, xh_grouped, copy):
            copy(
                out=xh_grouped[:, s, :, :].rearrange("p (w i) j -> p w j i", i=RUN),
                in_=xh_rows[:, b, s, :, :].rearrange("p j (w i) -> p w j i", i=RUN),
            )

        def quantise_features(b, xh_grouped):
            nc.vector.quantize_mx(
                out=xh_codes[:, b, :].bitcast(FP8X4),
                scales=xh_scales[:, b, :],
                in_=xh_grouped[:].rearrange("p s w j -> p (s w j)"),
            )

        def prepare(b):
            xh_grouped = stage.tile([P, SOURCES, HALF, PACK], BF16, align_bytes=64)
            for s in range(SOURCES):
                regroup_source(b, s, xh_grouped, nc.vector.tensor_copy)
            quantise_features(b, xh_grouped)

        def passes(b, codes, scales):
            banks = []
            for i in range(PACK):
                acc = psum.tile([P, WIDTH], F32, tag="bank")
                nc.tensor.matmul_mx(
                    out=acc[:],
                    lhsT=codes[:, quarter(i)].bitcast(FP8X4),
                    lhsT_scale=scales[:, quarter(i)],
                    rhs=xh_codes[:, b, :].bitcast(FP8X4),
                    rhs_scale=xh_scales[:, b, :],
                    start=True,
                    stop=True,
                )
                banks.append(acc)
            return banks

        def empty(banks, result, i, copy):
            copy(
                out=result[:, i],
                in_=banks[i][:].rearrange("r (s c d) -> r c s d", s=SOURCES, c=CHANNELS),
            )

        def store(out, b, result, first, count):
            span = slice(first * WIDTH, (first + count) * WIDTH)
            nc.sync.dma_start(
                out=out[b].rearrange("(r i) c l -> r (i c l)", i=PACK)[:, span],
                in_=result[:].rearrange("r i c s d -> r (i c s d)")[:, span],
            )

        def leave(out, b, banks, vector_banks, pieces=1):
            result = results.tile([P, PACK, CHANNELS, SOURCES, DIN], F32, align_bytes=256)
            step = PACK // pieces
            for i in range(PACK):
                empty(banks, result, i, nc.vector.tensor_copy if i in vector_banks else nc.scalar.copy)
                if (i + 1) % step == 0:
                    store(out, b, result, i + 1 - step, step)

        def x1(b):
            return passes(b, g_codes, g_scales)

        def x2(b):
            return passes(b, t2_codes, t2_scales)

        nc.vector.tensor_copy(
            out=g_grouped[:].rearrange("p i r j -> p r j i"),
            in_=g_rows[:].rearrange("p j (r i) -> p r j i", i=PACK),
        )
        first_grouped = stage.tile([P, SOURCES, HALF, PACK], BF16, align_bytes=64, tag="xh_grouped")
        second_grouped = stage.tile([P, SOURCES, HALF, PACK], BF16, align_bytes=64, tag="xh_grouped")
        regroup_source(0, 0, first_grouped, nc.scalar.copy)
        flip_graph()
        regroup_source(1, 0, second_grouped, nc.scalar.copy)
        regroup_source(0, 1, first_grouped, nc.vector.tensor_copy)
        nc.vector.quantize_mx(
            out=g_codes[:].bitcast(FP8X4),
            scales=g_scales[:],
            in_=g_grouped[:].rearrange("p i r j -> p (i r j)"),
        )
        quantise_features(0, first_grouped)
        leave(out_0, 0, x1(0), (), pieces=2)
        regroup_source(1, 1, second_grouped, nc.vector.tensor_copy)
        nc.vector.quantize_mx(out=gt_codes[:].bitcast(FP8X4), scales=gt_scales[:], in_=gt_grouped[:])
        quantise_features(1, second_grouped)
        squares = [square_graph(i) for i in range(PACK)]
        x1_banks = x1(1)
        for i in range(PACK + 1):
            if i < PACK:
                chebyshev(i, squares[i])
            if i > 0:
                quantise_chebyshev(i - 1)
        leave(out_0, 1, x1_banks, (), pieces=2)
        x2_banks = [x2(0), x2(1)]
        leave(out_1, 0, x2_banks[0], (0, 2))
        prepare(2)
        leave(out_1, 1, x2_banks[1], ())
        for b in range(2, PAIRS_FROM):
            leave(out_0, b, x1(b), ())
            prepare(b + 1)
            leave(out_1, b, x2(b), (0, 1))

        def store_pair(out, b, double):
            nc.sync.dma_start(
                out=out[b : b + 2].rearrange("b (r i) c l -> r b (i c l)", i=PACK),
                in_=double[:].rearrange("r b i c s d -> r b (i c s d)"),
            )

        for b in range(PAIRS_FROM, BATCH, 2):
            double = doubles.tile([P, 2, PACK, CHANNELS, SOURCES, DIN], F32, align_bytes=256)
            banks = x1(b)
            prepare(b + 1)
            for i in range(PACK):
                empty(banks, double[:, 0], i, nc.scalar.copy)
            banks = x1(b + 1)
            for i in range(PACK):
                empty(banks, double[:, 1], i, nc.scalar.copy)
            store_pair(out_0, b, double)
            double = doubles.tile([P, 2, PACK, CHANNELS, SOURCES, DIN], F32, align_bytes=256)
            banks = x2(b)
            for i in range(PACK):
                empty(banks, double[:, 0], i, nc.vector.tensor_copy if i < 2 else nc.scalar.copy)
            if b + 2 < BATCH:
                prepare(b + 2)
            banks = x2(b + 1)
            for i in range(PACK):
                empty(banks, double[:, 1], i, nc.vector.tensor_copy if i < 2 else nc.scalar.copy)
            store_pair(out_1, b, double)
